import numpy as np
import ml_dtypes


def mxq(x, axis, fmt="e4m3"):
    dtype, down = {"e4m3": (ml_dtypes.float8_e4m3fn, 7), "e5m2": (ml_dtypes.float8_e5m2, 14)}[fmt]
    v = np.moveaxis(np.asarray(x, np.float32).astype(ml_dtypes.bfloat16).astype(np.float64), axis, -1)
    blocks = v.reshape(v.shape[:-1] + (-1, 32))
    amax = np.abs(blocks).max(-1, keepdims=True)
    byte = np.maximum(np.where(amax > 0, np.frexp(amax)[1] - 1 + 127, 0) - down, 1)
    scale = np.exp2(byte - 127.0)
    codes = (blocks / scale).astype(np.float32).astype(dtype).astype(np.float64)
    return np.moveaxis((codes * scale).reshape(v.shape), -1, axis)


WIDE = False


def mx_kscale(k):
    if not WIDE:
        return np.ones(k)
    levels = np.array([10, -10, 5, -5, 0])
    if k % 512:
        return np.exp2(np.random.permutation(np.resize(levels, k // 32))).repeat(32)
    a = np.empty((k // 512, 16))
    for p in range(k // 512):
        a[p, :8] = np.random.permutation(np.resize(levels, 8))
        for g in range(8):
            far = levels[np.abs(levels - a[p, g]) >= 10]
            a[p, g + 8] = far[np.random.randint(len(far))]
    return np.exp2(a.ravel()).repeat(32)


BF16 = ml_dtypes.bfloat16


def bf(x):
    return np.asarray(x, np.float32).astype(BF16)


def f64(x):
    return np.asarray(x).astype(np.float64)


B, S, D, A0, A1, A2 = 2, 128, 4096, 64, 32, 128
AM = min(A0, A1, A2)


def kron(a, b):
    return (a[:, None, :, None] * b[None, :, None, :]).reshape(a.shape[0] * b.shape[0], a.shape[1] * b.shape[1])


def setup_inputs():
    u = mx_kscale(D)[:: D // AM]
    s = np.repeat(u, D // AM)
    inp = {"x": bf(np.random.standard_normal((B, S, D)) * s)}
    for i, a in enumerate((A0, A1, A2)):
        inp[f"L{i}"] = bf(np.random.uniform(size=(a, a)) / np.repeat(u, a // AM)[:, None])
        inp[f"R{i}"] = bf(np.random.uniform(size=(D // a, D // a)) * 3.0 / np.sqrt(D))
    inp["bias"] = bf(np.random.uniform(size=D))
    return inp


def reference(x, L0, R0, L1, R1, L2, R2, bias):
    pairs = [(f64(L0), f64(R0)), (f64(L1), f64(R1)), (f64(L2), f64(R2))]
    W = kron(pairs[0][0], pairs[0][1])
    for l, r in pairs[1:]:
        W = W + kron(l, r)
    W = W / len(pairs)
    return (mxq(f64(x), 2, "e4m3") @ mxq(W, 0, "e4m3")) + f64(bias)

@@ -1,0 +1,252 @@
+from contextlib import ExitStack
+
+import concourse.mybir as mybir
+from concourse.masks import make_identity
+
+F32 = mybir.dt.float32
+BF16 = mybir.dt.bfloat16
+U32 = mybir.dt.uint32
+U8 = mybir.dt.uint8
+FP8X4 = mybir.dt.float8_e4m3fn_x4
+MULT = mybir.AluOpType.mult
+ADD = mybir.AluOpType.add
+COPY = mybir.ActivationFunctionType.Copy
+
+P = 128
+D = 4096
+TOKENS = 256
+TOKEN_TILES = TOKENS // P
+PACK = 4
+PASSES = D // (P * PACK)
+UNITS = 32
+UNIT_COLS = D // UNITS
+RUN = UNIT_COLS * PACK
+UNIT = PASSES * RUN
+GROUP = 4
+GROUPS = UNITS // GROUP
+QUANT_IN = 4096
+GPSIMD_UNITS_OF_16 = 9
+
+L2_AT, L0_AT, L1_AT, L_COLS = 0, 1024, 1280, 1344
+R1_AT, R0_AT, R2_AT, R_COLS = 0, 2048, 2560, 2688
+
+FLOPS = 2 * TOKENS * D * D
+
+
+def tile_klinear_kernel(tc, x, L0, R0, L1, R1, L2, R2, bias, out):
+    nc = tc.nc
+    x_rows = x.flatten_outer_dims()
+    out_rows = out.flatten_outer_dims()
+
+    with ExitStack() as pools:
+        keep = pools.enter_context(tc.tile_pool(name="keep", bufs=1))
+        partials = pools.enter_context(tc.tile_pool(name="partials", bufs=4))
+        products = pools.enter_context(tc.tile_pool(name="products", bufs=3))
+        blocks = pools.enter_context(tc.tile_pool(name="blocks", bufs=3))
+        results = pools.enter_context(tc.tile_pool(name="results", bufs=2))
+        stage = pools.enter_context(tc.tile_pool(name="stage", bufs=1))
+        r_psum = pools.enter_context(tc.psum_pool(name="r_psum", bufs=1))
+        xt_pool = pools.enter_context(tc.psum_pool(name="xt", bufs=1))
+        acc_pool = pools.enter_context(tc.psum_pool(name="acc", bufs=2))
+
+        l_raw = stage.tile([P, L_COLS], BF16)
+        r_raw = stage.tile([P, R_COLS], BF16)
+        nc.vector.memset(l_raw[:].bitcast(U32), 0)
+        nc.gpsimd.memset(r_raw[:].bitcast(U32), 0)
+        nc.sync.dma_start(out=l_raw[0:16, L2_AT:L0_AT], in_=L2.rearrange("(g c) n -> g (c n)", c=8))
+        nc.scalar.dma_start(out=r_raw[0:8, R2_AT:R_COLS], in_=R2.rearrange("(i t) n -> i (t n)", t=PACK))
+        nc.sync.dma_start(out=l_raw[0:16, L0_AT:L1_AT], in_=L0.rearrange("(g c) n -> g (c n)", c=4))
+        nc.scalar.dma_start(
+            out=r_raw[0:8, R0_AT:R2_AT].rearrange("p (c j) -> p c j", c=2),
+            in_=R0.rearrange("(c i t) n -> i c (t n)", c=2, t=PACK),
+        )
+        nc.sync.dma_start(out=l_raw[0:16, L1_AT:L_COLS], in_=L1.rearrange("(g c) n -> g (c n)", c=2))
+        nc.scalar.dma_start(
+            out=r_raw[0:8, R1_AT:R0_AT].rearrange("p (c j) -> p c j", c=4),
+            in_=R1.rearrange("(c i t) n -> i c (t n)", c=4, t=PACK),
+        )
+        x_sb = stage.tile([P, TOKEN_TILES, D], BF16, align_bytes=64, tag="x_a")
+        for m in range(TOKEN_TILES):
+            nc.sync.dma_start(out=x_sb[:, m, :], in_=x_rows[m * P : (m + 1) * P, :])
+        bias_all = keep.tile([P, D], BF16)
+        nc.sync.dma_start(out=bias_all[:], in_=bias.partition_broadcast(P))
+
+        ident = keep.tile([P, P], F32)
+        make_identity(nc, ident[:])
+        spread_l = keep.tile([P, P], BF16)
+        spread_r = keep.tile([P, P], BF16)
+        nc.vector.tensor_copy(
+            out=spread_l[:].rearrange("k (g i) -> k g i", i=8), in_=ident[:, 0:16].unsqueeze(2).to_broadcast([P, 16, 8])
+        )
+        nc.vector.tensor_copy(
+            out=spread_r[:].rearrange("k (g i) -> k g i", i=8), in_=ident[:, 0:8].unsqueeze(1).to_broadcast([P, 16, 8])
+        )
+
+        l_third = keep.tile([P, L_COLS], F32)
+        r_small = keep.tile([P, R_COLS - R0_AT], BF16)
+        r1_banks = [r_psum.tile([P, 2 * RUN], BF16, name="r1_bank%d" % h) for h in range(2)]
+        r0_bank = r_psum.tile([P, 1024], BF16)
+
+        def spread_l_cols(tag, at, width):
+            bank = acc_pool.tile([P, 512], F32, name=tag)
+            nc.tensor.matmul(out=bank[:, :width], lhsT=spread_l[:], rhs=l_raw[:, at : at + width], start=True, stop=True)
+            nc.scalar.activation(out=l_third[:, at : at + width], in_=bank[:, :width], func=COPY, scale=1.0 / 3.0)
+
+        def spread_r_rows(bank_cols, at, cols):
+            nc.tensor.matmul(
+                out=bank_cols,
+                lhsT=spread_r[:],
+                rhs=r_raw[:, at : at + PACK * cols].rearrange("p (t n) -> p n t", t=PACK),
+                start=True,
+                stop=True,
+            )
+
+        spread_r_rows(r0_bank[:, 512:640], R2_AT, 32)
+        spread_l_cols("acc0", 0, 512)
+        spread_l_cols("acc1", 512, 512)
+        for h in range(2):
+            spread_r_rows(r0_bank[:, 256 * h : 256 * (h + 1)], R0_AT + 256 * h, 64)
+        nc.vector.tensor_copy(out=r_small[:], in_=r0_bank[:, 0:640])
+        spread_l_cols("acc0", L0_AT, L_COLS - L0_AT)
+        for h in range(4):
+            spread_r_rows(r1_banks[h // 2][:, RUN * (h % 2) : RUN * (h % 2 + 1)], R1_AT + RUN * h, UNIT_COLS)
+
+        x_codes = keep.tile([P, PASSES * TOKENS], U32, align_bytes=64)
+        x_scales = keep.tile([P, PASSES * TOKENS], U8, align_bytes=64)
+
+        def prepare_x():
+            x_words = stage.tile([P, TOKEN_TILES, 2, D // 4], F32)
+            for m in range(TOKEN_TILES):
+                by_u = x_sb[:, m, :].bitcast(F32).rearrange("p (g c i u) -> p u c g i", c=8, i=8, u=2)
+                for u in range(2):
+                    nc.vector.tensor_copy(
+                        out=x_words[:, m, u, :].rearrange("p (c g i) -> p c g i", c=8, i=8), in_=by_u[:, u]
+                    )
+            x_grouped = stage.tile([P, PASSES, TOKENS * PACK], BF16, align_bytes=64, tag="x_a")
+            for c in range(PASSES):
+                x_t = xt_pool.tile([P, 2, TOKENS], F32)
+                for u in range(2):
+                    for m in range(TOKEN_TILES):
+                        nc.tensor.transpose(
+                            x_t[:, u, m * P : (m + 1) * P], x_words[:, m, u, c * P : (c + 1) * P], ident[:]
+                        )
+                nc.scalar.copy(
+                    out=x_grouped[:, c, :].bitcast(F32).rearrange("p (r u) -> p r u", u=2),
+                    in_=x_t[:].rearrange("p u r -> p r u"),
+                )
+            x_flat = x_grouped[:].rearrange("p c j -> p (c j)")
+            for h in range(PASSES * TOKENS * PACK // QUANT_IN):
+                words = slice(h * QUANT_IN // PACK, (h + 1) * QUANT_IN // PACK)
+                nc.vector.quantize_mx(
+                    out=x_codes[:, words].bitcast(FP8X4),
+                    scales=x_scales[:, words],
+                    in_=x_flat[:, h * QUANT_IN : (h + 1) * QUANT_IN],
+                )
+
+        def l_scalar(at):
+            return l_third[:, at : at + 1]
+
+        def by_half(tile_ap, c2, f):
+            return tile_ap.rearrange("p (a h f j) -> p a h f j", h=2, f=2, j=256)[:, c2, :, f, :]
+
+        def build_partial(b):
+            partial = partials.tile([P, UNIT], F32)
+            for c in range(PASSES):
+                for fg in range(4):
+                    at = c * RUN + fg * 128
+                    nc.scalar.activation(
+                        out=partial[:, at : at + 128],
+                        in_=r_small[:, 512:640],
+                        func=COPY,
+                        scale=l_scalar(L2_AT + c * 128 + 4 * b + fg),
+                    )
+            r0_row = r0_bank[:, 0:512].rearrange("p (h j) -> p h j", h=2)
+            if (b * GPSIMD_UNITS_OF_16) % 16 < GPSIMD_UNITS_OF_16:
+                product = products.tile([P, UNIT], F32)
+                for c2 in range(4):
+                    for f in range(2):
+                        nc.scalar.activation(
+                            out=by_half(product[:], c2, f),
+                            in_=r_small[:, 0:512].rearrange("p (h j) -> p h j", h=2),
+                            func=COPY,
+                            scale=l_scalar(L0_AT + c2 * 64 + 2 * b + f),
+                        )
+                for h in range(2):
+                    half = slice(h * UNIT // 2, (h + 1) * UNIT // 2)
+                    nc.gpsimd.tensor_tensor(out=partial[:, half], in0=partial[:, half], in1=product[:, half], op=ADD)
+            else:
+                for c2 in range(4):
+                    for f in range(2):
+                        nc.vector.scalar_tensor_tensor(
+                            out=by_half(partial[:], c2, f),
+                            in0=r0_row,
+                            scalar=l_scalar(L0_AT + c2 * 64 + 2 * b + f),
+                            in1=by_half(partial[:], c2, f),
+                            op0=MULT,
+                            op1=ADD,
+                        )
+            return partial
+
+        def add_last(w_bf16, partial, b, c_hi):
+            for h in range(2):
+                cols = slice((2 * c_hi + h) * 2 * RUN, (2 * c_hi + h + 1) * 2 * RUN)
+                nc.vector.scalar_tensor_tensor(
+                    out=w_bf16[:, cols],
+                    in0=r1_banks[h][:],
+                    scalar=l_scalar(L1_AT + c_hi * 32 + b),
+                    in1=partial[:, cols],
+                    op0=MULT,
+                    op1=ADD,
+                )
+
+        def quantise(w_bf16):
+            w_codes = blocks.tile([P, PASSES * UNIT_COLS], U32, align_bytes=64)
+            w_scales = blocks.tile([P, PASSES * UNIT_COLS], U8, align_bytes=64)
+            nc.vector.quantize_mx(out=w_codes[:].bitcast(FP8X4), scales=w_scales[:], in_=w_bf16[:])
+            return w_codes, w_scales
+
+        def multiply(acc, b, w_codes, w_scales):
+            for m in range(TOKEN_TILES):
+                for c in range(PASSES):
+                    x_cols = slice(c * TOKENS + m * P, c * TOKENS + (m + 1) * P)
+                    w_cols = slice(c * UNIT_COLS, (c + 1) * UNIT_COLS)
+                    nc.tensor.matmul_mx(
+                        out=acc[m][:, (b % GROUP) * UNIT_COLS : (b % GROUP + 1) * UNIT_COLS],
+                        lhsT=x_codes[:, x_cols].bitcast(FP8X4),
+                        lhsT_scale=x_scales[:, x_cols],
+                        rhs=w_codes[:, w_cols].bitcast(FP8X4),
+                        rhs_scale=w_scales[:, w_cols],
+                        start=(c == 0),
+                        stop=(c == PASSES - 1),
+                    )
+
+        def finish(acc, q):
+            cols = slice(q * GROUP * UNIT_COLS, (q + 1) * GROUP * UNIT_COLS)
+            for m in range(TOKEN_TILES):
+                result = results.tile([P, GROUP * UNIT_COLS], F32, name="result%d" % m)
+                nc.vector.tensor_tensor(out=result[:], in0=acc[m][:], in1=bias_all[:, cols], op=ADD)
+                nc.sync.dma_start(out=out_rows[m * P : (m + 1) * P, cols], in_=result[:])
+
+        accs = {}
+        last = None
+
+        def quantise_and_multiply(b, w_bf16):
+            if b % GROUP == 0:
+                accs[b // GROUP] = [acc_pool.tile([P, GROUP * UNIT_COLS], F32, name="acc%d" % m) for m in range(2)]
+            w_codes, w_scales = quantise(w_bf16)
+            multiply(accs[b // GROUP], b, w_codes, w_scales)
+
+        for b in range(UNITS):
+            partial = build_partial(b)
+            w_bf16 = blocks.tile([P, UNIT], BF16, align_bytes=64)
+            add_last(w_bf16, partial, b, 0)
+            if b == 1:
+                prepare_x()
+            if b > 0:
+                quantise_and_multiply(b - 1, last)
+            add_last(w_bf16, partial, b, 1)
+            if b % GROUP == 2 and b > GROUP:
+                finish(accs[b // GROUP - 1], b // GROUP - 1)
+            last = w_bf16
+        quantise_and_multiply(UNITS - 1, last)
+        finish(accs[GROUPS - 1], GROUPS - 1)

@@ -25,7 +25,8 @@ UNIT = PASSES * RUN
 GROUP = 4
 GROUPS = UNITS // GROUP
 QUANT_IN = 4096
-GPSIMD_UNITS_OF_16 = 9
+GP_BLOCKS = 5
+GP_PRODUCTS = 1
 
 L2_AT, L0_AT, L1_AT, L_COLS = 0, 1024, 1280, 1344
 R1_AT, R0_AT, R2_AT, R_COLS = 0, 2048, 2560, 2688
@@ -48,11 +49,14 @@ def tile_klinear_kernel(tc, x, L0, R0, L1, R1, L2, R2, bias, out):
         r_psum = pools.enter_context(tc.psum_pool(name="r_psum", bufs=1))
         xt_pool = pools.enter_context(tc.psum_pool(name="xt", bufs=1))
         acc_pool = pools.enter_context(tc.psum_pool(name="acc", bufs=2))
+        pools.enter_context(tc.manual_schedule())
 
         l_raw = stage.tile([P, L_COLS], BF16)
         r_raw = stage.tile([P, R_COLS], BF16)
+        ident = keep.tile([P, P], F32)
         nc.vector.memset(l_raw[:].bitcast(U32), 0)
-        nc.gpsimd.memset(r_raw[:].bitcast(U32), 0)
+        nc.vector.memset(r_raw[:].bitcast(U32), 0)
+        make_identity(nc, ident[:])
         nc.sync.dma_start(out=l_raw[0:16, L2_AT:L0_AT], in_=L2.rearrange("(g c) n -> g (c n)", c=8))
         nc.scalar.dma_start(out=r_raw[0:8, R2_AT:R_COLS], in_=R2.rearrange("(i t) n -> i (t n)", t=PACK))
         nc.sync.dma_start(out=l_raw[0:16, L0_AT:L1_AT], in_=L0.rearrange("(g c) n -> g (c n)", c=4))
@@ -71,8 +75,6 @@ def tile_klinear_kernel(tc, x, L0, R0, L1, R1, L2, R2, bias, out):
         bias_all = keep.tile([P, D], BF16)
         nc.sync.dma_start(out=bias_all[:], in_=bias.partition_broadcast(P))
 
-        ident = keep.tile([P, P], F32)
-        make_identity(nc, ident[:])
         spread_l = keep.tile([P, P], BF16)
         spread_r = keep.tile([P, P], BF16)
         nc.vector.tensor_copy(
@@ -90,6 +92,9 @@ def tile_klinear_kernel(tc, x, L0, R0, L1, R1, L2, R2, bias, out):
         def spread_l_cols(tag, at, width):
             bank = acc_pool.tile([P, 512], F32, name=tag)
             nc.tensor.matmul(out=bank[:, :width], lhsT=spread_l[:], rhs=l_raw[:, at : at + width], start=True, stop=True)
+            return bank
+
+        def third_on_scalar(bank, at, width):
             nc.scalar.activation(out=l_third[:, at : at + width], in_=bank[:, :width], func=COPY, scale=1.0 / 3.0)
 
         def spread_r_rows(bank_cols, at, cols):
@@ -101,27 +106,32 @@ def tile_klinear_kernel(tc, x, L0, R0, L1, R1, L2, R2, bias, out):
                 stop=True,
             )
 
+        bank0 = spread_l_cols("acc0", 0, 512)
+        bank1 = spread_l_cols("acc1", 512, 512)
         spread_r_rows(r0_bank[:, 512:640], R2_AT, 32)
-        spread_l_cols("acc0", 0, 512)
-        spread_l_cols("acc1", 512, 512)
         for h in range(2):
             spread_r_rows(r0_bank[:, 256 * h : 256 * (h + 1)], R0_AT + 256 * h, 64)
+        third_on_scalar(bank0, 0, 512)
+        nc.vector.tensor_scalar_mul(out=l_third[:, 512:1024], in0=bank1[:], scalar1=1.0 / 3.0)
         nc.vector.tensor_copy(out=r_small[:], in_=r0_bank[:, 0:640])
-        spread_l_cols("acc0", L0_AT, L_COLS - L0_AT)
+        bank2 = spread_l_cols("acc0", L0_AT, L_COLS - L0_AT)
+        nc.vector.tensor_scalar_mul(out=l_third[:, L0_AT:L_COLS], in0=bank2[:, : L_COLS - L0_AT], scalar1=1.0 / 3.0)
         for h in range(4):
             spread_r_rows(r1_banks[h // 2][:, RUN * (h % 2) : RUN * (h % 2 + 1)], R1_AT + RUN * h, UNIT_COLS)
 
         x_codes = keep.tile([P, PASSES * TOKENS], U32, align_bytes=64)
         x_scales = keep.tile([P, PASSES * TOKENS], U8, align_bytes=64)
+        x_words = stage.tile([P, TOKEN_TILES, 2, D // 4], F32)
 
-        def prepare_x():
-            x_words = stage.tile([P, TOKEN_TILES, 2, D // 4], F32)
+        def order_x():
             for m in range(TOKEN_TILES):
                 by_u = x_sb[:, m, :].bitcast(F32).rearrange("p (g c i u) -> p u c g i", c=8, i=8, u=2)
                 for u in range(2):
                     nc.vector.tensor_copy(
                         out=x_words[:, m, u, :].rearrange("p (c g i) -> p c g i", c=8, i=8), in_=by_u[:, u]
                     )
+
+        def turn_x():
             x_grouped = stage.tile([P, PASSES, TOKENS * PACK], BF16, align_bytes=64, tag="x_a")
             for c in range(PASSES):
                 x_t = xt_pool.tile([P, 2, TOKENS], F32)
@@ -134,6 +144,9 @@ def tile_klinear_kernel(tc, x, L0, R0, L1, R1, L2, R2, bias, out):
                     out=x_grouped[:, c, :].bitcast(F32).rearrange("p (r u) -> p r u", u=2),
                     in_=x_t[:].rearrange("p u r -> p r u"),
                 )
+            return x_grouped
+
+        def quantise_x(x_grouped):
             x_flat = x_grouped[:].rearrange("p c j -> p (c j)")
             for h in range(PASSES * TOKENS * PACK // QUANT_IN):
                 words = slice(h * QUANT_IN // PACK, (h + 1) * QUANT_IN // PACK)
@@ -146,10 +159,25 @@ def tile_klinear_kernel(tc, x, L0, R0, L1, R1, L2, R2, bias, out):
         def l_scalar(at):
             return l_third[:, at : at + 1]
 
-        def by_half(tile_ap, c2, f):
-            return tile_ap.rearrange("p (a h f j) -> p a h f j", h=2, f=2, j=256)[:, c2, :, f, :]
+        def l0_scalar(b, j):
+            return l_scalar(L0_AT + (j // 2) * 64 + 2 * b + j % 2)
 
-        def build_partial(b):
+        def block_of(tile_ap, j):
+            return tile_ap.rearrange("p (a h f j) -> p a h f j", h=2, f=2, j=256)[:, j // 2, :, j % 2, :]
+
+        r0_row = r_small[:, 0:512].rearrange("p (h j) -> p h j", h=2)
+        r0_psum_row = r0_bank[:, 0:512].rearrange("p (h j) -> p h j", h=2)
+        partial_of, product_of, w_of, code_of, accs = {}, {}, {}, {}, {}
+
+        def gp_blocks(b):
+            return 0 if b == 0 else GP_BLOCKS
+
+        def product_cols(product, j):
+            if j < 4:
+                return block_of(product[:, 0 : UNIT // 2], j)
+            return product[:, UNIT // 2 :].rearrange("p (h j) -> p h j", h=2)
+
+        def scalar_products(b):
             partial = partials.tile([P, UNIT], F32)
             for c in range(PASSES):
                 for fg in range(4):
@@ -160,52 +188,65 @@ def tile_klinear_kernel(tc, x, L0, R0, L1, R1, L2, R2, bias, out):
                         func=COPY,
                         scale=l_scalar(L2_AT + c * 128 + 4 * b + fg),
                     )
-            r0_row = r0_bank[:, 0:512].rearrange("p (h j) -> p h j", h=2)
-            if (b * GPSIMD_UNITS_OF_16) % 16 < GPSIMD_UNITS_OF_16:
-                product = products.tile([P, UNIT], F32)
-                for c2 in range(4):
-                    for f in range(2):
-                        nc.scalar.activation(
-                            out=by_half(product[:], c2, f),
-                            in_=r_small[:, 0:512].rearrange("p (h j) -> p h j", h=2),
-                            func=COPY,
-                            scale=l_scalar(L0_AT + c2 * 64 + 2 * b + f),
-                        )
-                for h in range(2):
-                    half = slice(h * UNIT // 2, (h + 1) * UNIT // 2)
-                    nc.gpsimd.tensor_tensor(out=partial[:, half], in0=partial[:, half], in1=product[:, half], op=ADD)
-            else:
-                for c2 in range(4):
-                    for f in range(2):
-                        nc.vector.scalar_tensor_tensor(
-                            out=by_half(partial[:], c2, f),
-                            in0=r0_row,
-                            scalar=l_scalar(L0_AT + c2 * 64 + 2 * b + f),
-                            in1=by_half(partial[:], c2, f),
-                            op0=MULT,
-                            op1=ADD,
-                        )
-            return partial
+            partial_of[b] = partial
+            if gp_blocks(b):
+                product = products.tile([P, UNIT // 2 + 512], F32)
+                for j in range(GP_BLOCKS - GP_PRODUCTS):
+                    nc.scalar.activation(out=product_cols(product, j), in_=r0_row, func=COPY, scale=l0_scalar(b, j))
+                product_of[b] = product
 
-        def add_last(w_bf16, partial, b, c_hi):
-            for h in range(2):
-                cols = slice((2 * c_hi + h) * 2 * RUN, (2 * c_hi + h + 1) * 2 * RUN)
+        def gpsimd_sums(b):
+            if not gp_blocks(b):
+                return
+            partial, product = partial_of[b], product_of[b]
+            for j in range(GP_BLOCKS - GP_PRODUCTS, GP_BLOCKS):
+                nc.gpsimd.tensor_scalar(
+                    out=product_cols(product, j), in0=r0_row, scalar1=l0_scalar(b, j), scalar2=0.0, op0=MULT, op1=ADD
+                )
+            half = slice(0, UNIT // 2)
+            nc.gpsimd.tensor_tensor(out=partial[:, half], in0=partial[:, half], in1=product[:, half], op=ADD)
+            nc.gpsimd.tensor_tensor(
+                out=block_of(partial[:], 4), in0=block_of(partial[:], 4), in1=product_cols(product, 4), op=ADD
+            )
+
+        def vector_sums(b):
+            partial = partial_of[b]
+            for j in range(gp_blocks(b), 8):
                 nc.vector.scalar_tensor_tensor(
-                    out=w_bf16[:, cols],
-                    in0=r1_banks[h][:],
-                    scalar=l_scalar(L1_AT + c_hi * 32 + b),
-                    in1=partial[:, cols],
+                    out=block_of(partial[:], j),
+                    in0=r0_psum_row,
+                    scalar=l0_scalar(b, j),
+                    in1=block_of(partial[:], j),
                     op0=MULT,
                     op1=ADD,
                 )
 
-        def quantise(w_bf16):
+        def add_last(b):
+            w_bf16 = blocks.tile([P, UNIT], BF16, align_bytes=64)
+            for c_hi in range(2):
+                for h in range(2):
+                    cols = slice((2 * c_hi + h) * 2 * RUN, (2 * c_hi + h + 1) * 2 * RUN)
+                    nc.vector.scalar_tensor_tensor(
+                        out=w_bf16[:, cols],
+                        in0=r1_banks[h][:],
+                        scalar=l_scalar(L1_AT + c_hi * 32 + b),
+                        in1=partial_of[b][:, cols],
+                        op0=MULT,
+                        op1=ADD,
+                    )
+            w_of[b] = w_bf16
+
+        def quantise(b):
             w_codes = blocks.tile([P, PASSES * UNIT_COLS], U32, align_bytes=64)
             w_scales = blocks.tile([P, PASSES * UNIT_COLS], U8, align_bytes=64)
-            nc.vector.quantize_mx(out=w_codes[:].bitcast(FP8X4), scales=w_scales[:], in_=w_bf16[:])
-            return w_codes, w_scales
+            nc.vector.quantize_mx(out=w_codes[:].bitcast(FP8X4), scales=w_scales[:], in_=w_of[b][:])
+            code_of[b] = (w_codes, w_scales)
 
-        def multiply(acc, b, w_codes, w_scales):
+        def multiply(b):
+            if b % GROUP == 0:
+                accs[b // GROUP] = [acc_pool.tile([P, GROUP * UNIT_COLS], F32, name="acc%d" % m) for m in range(2)]
+            acc = accs[b // GROUP]
+            w_codes, w_scales = code_of[b]
             for m in range(TOKEN_TILES):
                 for c in range(PASSES):
                     x_cols = slice(c * TOKENS + m * P, c * TOKENS + (m + 1) * P)
@@ -220,33 +261,39 @@ def tile_klinear_kernel(tc, x, L0, R0, L1, R1, L2, R2, bias, out):
                         stop=(c == PASSES - 1),
                     )
 
-        def finish(acc, q):
+        def finish(q):
             cols = slice(q * GROUP * UNIT_COLS, (q + 1) * GROUP * UNIT_COLS)
             for m in range(TOKEN_TILES):
                 result = results.tile([P, GROUP * UNIT_COLS], F32, name="result%d" % m)
-                nc.vector.tensor_tensor(out=result[:], in0=acc[m][:], in1=bias_all[:, cols], op=ADD)
+                nc.vector.tensor_tensor(out=result[:], in0=accs[q][m][:], in1=bias_all[:, cols], op=ADD)
                 nc.sync.dma_start(out=out_rows[m * P : (m + 1) * P, cols], in_=result[:])
 
-        accs = {}
-        last = None
+        turnstile = keep.tile([P, 1], U32)
 
-        def quantise_and_multiply(b, w_bf16):
-            if b % GROUP == 0:
-                accs[b // GROUP] = [acc_pool.tile([P, GROUP * UNIT_COLS], F32, name="acc%d" % m) for m in range(2)]
-            w_codes, w_scales = quantise(w_bf16)
-            multiply(accs[b // GROUP], b, w_codes, w_scales)
+        def gpsimd_after_quantise(b):
+            nc.gpsimd.tensor_copy(out=turnstile[:], in_=code_of[b][0][:, 0:1])
 
+        order_x()
+        scalar_products(0)
+        scalar_products(1)
         for b in range(UNITS):
-            partial = build_partial(b)
-            w_bf16 = blocks.tile([P, UNIT], BF16, align_bytes=64)
-            add_last(w_bf16, partial, b, 0)
-            if b == 1:
-                prepare_x()
+            if b == 0:
+                x_grouped = turn_x()
+            if b + 2 < UNITS:
+                scalar_products(b + 2)
+            vector_sums(b)
             if b > 0:
-                quantise_and_multiply(b - 1, last)
-            add_last(w_bf16, partial, b, 1)
+                quantise(b - 1)
+                gpsimd_after_quantise(b - 1)
+            if b + 1 < UNITS:
+                gpsimd_sums(b + 1)
+            if b == 1:
+                quantise_x(x_grouped)
+            add_last(b)
+            if b > 0:
+                multiply(b - 1)
             if b % GROUP == 2 and b > GROUP:
-                finish(accs[b // GROUP - 1], b // GROUP - 1)
-            last = w_bf16
-        quantise_and_multiply(UNITS - 1, last)
-        finish(accs[GROUPS - 1], GROUPS - 1)
+                finish(b // GROUP - 1)
+        quantise(UNITS - 1)
+        multiply(UNITS - 1)
+        finish(GROUPS - 1)

@@ -25,8 +25,6 @@ UNIT = PASSES * RUN
 GROUP = 4
 GROUPS = UNITS // GROUP
 QUANT_IN = 4096
-GP_BLOCKS = 5
-GP_PRODUCTS = 1
 
 L2_AT, L0_AT, L1_AT, L_COLS = 0, 1024, 1280, 1344
 R1_AT, R0_AT, R2_AT, R_COLS = 0, 2048, 2560, 2688
@@ -170,7 +168,7 @@ def tile_klinear_kernel(tc, x, L0, R0, L1, R1, L2, R2, bias, out):
         partial_of, product_of, w_of, code_of, accs = {}, {}, {}, {}, {}
 
         def gp_blocks(b):
-            return 0 if b == 0 else GP_BLOCKS
+            return 0 if b == 0 else 4 + b % 2
 
         def product_cols(product, j):
             if j < 4:
@@ -191,7 +189,7 @@ def tile_klinear_kernel(tc, x, L0, R0, L1, R1, L2, R2, bias, out):
             partial_of[b] = partial
             if gp_blocks(b):
                 product = products.tile([P, UNIT // 2 + 512], F32)
-                for j in range(GP_BLOCKS - GP_PRODUCTS):
+                for j in range(gp_blocks(b)):
                     nc.scalar.activation(out=product_cols(product, j), in_=r0_row, func=COPY, scale=l0_scalar(b, j))
                 product_of[b] = product
 
@@ -199,15 +197,12 @@ def tile_klinear_kernel(tc, x, L0, R0, L1, R1, L2, R2, bias, out):
             if not gp_blocks(b):
                 return
             partial, product = partial_of[b], product_of[b]
-            for j in range(GP_BLOCKS - GP_PRODUCTS, GP_BLOCKS):
-                nc.gpsimd.tensor_scalar(
-                    out=product_cols(product, j), in0=r0_row, scalar1=l0_scalar(b, j), scalar2=0.0, op0=MULT, op1=ADD
-                )
             half = slice(0, UNIT // 2)
             nc.gpsimd.tensor_tensor(out=partial[:, half], in0=partial[:, half], in1=product[:, half], op=ADD)
-            nc.gpsimd.tensor_tensor(
-                out=block_of(partial[:], 4), in0=block_of(partial[:], 4), in1=product_cols(product, 4), op=ADD
-            )
+            if gp_blocks(b) > 4:
+                nc.gpsimd.tensor_tensor(
+                    out=block_of(partial[:], 4), in0=block_of(partial[:], 4), in1=product_cols(product, 4), op=ADD
+                )
 
         def vector_sums(b):
             partial = partial_of[b]

@@ -25,6 +25,7 @@ UNIT = PASSES * RUN
 GROUP = 4
 GROUPS = UNITS // GROUP
 QUANT_IN = 4096
+X_READY = 4
 
 L2_AT, L0_AT, L1_AT, L_COLS = 0, 1024, 1280, 1344
 R1_AT, R0_AT, R2_AT, R_COLS = 0, 2048, 2560, 2688
@@ -42,6 +43,7 @@ def tile_klinear_kernel(tc, x, L0, R0, L1, R1, L2, R2, bias, out):
         partials = pools.enter_context(tc.tile_pool(name="partials", bufs=4))
         products = pools.enter_context(tc.tile_pool(name="products", bufs=3))
         blocks = pools.enter_context(tc.tile_pool(name="blocks", bufs=3))
+        coded = pools.enter_context(tc.tile_pool(name="coded", bufs=6))
         results = pools.enter_context(tc.tile_pool(name="results", bufs=2))
         stage = pools.enter_context(tc.tile_pool(name="stage", bufs=1))
         r_psum = pools.enter_context(tc.psum_pool(name="r_psum", bufs=1))
@@ -52,18 +54,20 @@ def tile_klinear_kernel(tc, x, L0, R0, L1, R1, L2, R2, bias, out):
         l_raw = stage.tile([P, L_COLS], BF16)
         r_raw = stage.tile([P, R_COLS], BF16)
         ident = keep.tile([P, P], F32)
-        nc.vector.memset(l_raw[:].bitcast(U32), 0)
-        nc.vector.memset(r_raw[:].bitcast(U32), 0)
+        nc.vector.memset(l_raw[:, 0:L0_AT].bitcast(U32), 0)
+        nc.vector.memset(r_raw[:, R0_AT:].bitcast(U32), 0)
+        nc.vector.memset(l_raw[:, L0_AT:].bitcast(U32), 0)
         make_identity(nc, ident[:])
+        nc.gpsimd.memset(r_raw[:, :R0_AT].bitcast(U32), 0)
         nc.sync.dma_start(out=l_raw[0:16, L2_AT:L0_AT], in_=L2.rearrange("(g c) n -> g (c n)", c=8))
-        nc.scalar.dma_start(out=r_raw[0:8, R2_AT:R_COLS], in_=R2.rearrange("(i t) n -> i (t n)", t=PACK))
-        nc.sync.dma_start(out=l_raw[0:16, L0_AT:L1_AT], in_=L0.rearrange("(g c) n -> g (c n)", c=4))
-        nc.scalar.dma_start(
+        nc.sync.dma_start(out=r_raw[0:8, R2_AT:R_COLS], in_=R2.rearrange("(i t) n -> i (t n)", t=PACK))
+        nc.sync.dma_start(
             out=r_raw[0:8, R0_AT:R2_AT].rearrange("p (c j) -> p c j", c=2),
             in_=R0.rearrange("(c i t) n -> i c (t n)", c=2, t=PACK),
         )
+        nc.sync.dma_start(out=l_raw[0:16, L0_AT:L1_AT], in_=L0.rearrange("(g c) n -> g (c n)", c=4))
         nc.sync.dma_start(out=l_raw[0:16, L1_AT:L_COLS], in_=L1.rearrange("(g c) n -> g (c n)", c=2))
-        nc.scalar.dma_start(
+        nc.sync.dma_start(
             out=r_raw[0:8, R1_AT:R0_AT].rearrange("p (c j) -> p c j", c=4),
             in_=R1.rearrange("(c i t) n -> i c (t n)", c=4, t=PACK),
         )
@@ -107,9 +111,9 @@ def tile_klinear_kernel(tc, x, L0, R0, L1, R1, L2, R2, bias, out):
         bank0 = spread_l_cols("acc0", 0, 512)
         bank1 = spread_l_cols("acc1", 512, 512)
         spread_r_rows(r0_bank[:, 512:640], R2_AT, 32)
+        third_on_scalar(bank0, 0, 512)
         for h in range(2):
             spread_r_rows(r0_bank[:, 256 * h : 256 * (h + 1)], R0_AT + 256 * h, 64)
-        third_on_scalar(bank0, 0, 512)
         nc.vector.tensor_scalar_mul(out=l_third[:, 512:1024], in0=bank1[:], scalar1=1.0 / 3.0)
         nc.vector.tensor_copy(out=r_small[:], in_=r0_bank[:, 0:640])
         bank2 = spread_l_cols("acc0", L0_AT, L_COLS - L0_AT)
@@ -168,7 +172,7 @@ def tile_klinear_kernel(tc, x, L0, R0, L1, R1, L2, R2, bias, out):
         partial_of, product_of, w_of, code_of, accs = {}, {}, {}, {}, {}
 
         def gp_blocks(b):
-            return 0 if b == 0 else 4 + b % 2
+            return 0 if b < 2 else 4 + b % 2
 
         def product_cols(product, j):
             if j < 4:
@@ -232,8 +236,8 @@ def tile_klinear_kernel(tc, x, L0, R0, L1, R1, L2, R2, bias, out):
             w_of[b] = w_bf16
 
         def quantise(b):
-            w_codes = blocks.tile([P, PASSES * UNIT_COLS], U32, align_bytes=64)
-            w_scales = blocks.tile([P, PASSES * UNIT_COLS], U8, align_bytes=64)
+            w_codes = coded.tile([P, PASSES * UNIT_COLS], U32, align_bytes=64)
+            w_scales = coded.tile([P, PASSES * UNIT_COLS], U8, align_bytes=64)
             nc.vector.quantize_mx(out=w_codes[:].bitcast(FP8X4), scales=w_scales[:], in_=w_of[b][:])
             code_of[b] = (w_codes, w_scales)
 
@@ -272,20 +276,22 @@ def tile_klinear_kernel(tc, x, L0, R0, L1, R1, L2, R2, bias, out):
         scalar_products(0)
         scalar_products(1)
         for b in range(UNITS):
-            if b == 0:
-                x_grouped = turn_x()
             if b + 2 < UNITS:
                 scalar_products(b + 2)
+            if b == 1:
+                x_grouped = turn_x()
             vector_sums(b)
             if b > 0:
                 quantise(b - 1)
                 gpsimd_after_quantise(b - 1)
             if b + 1 < UNITS:
                 gpsimd_sums(b + 1)
-            if b == 1:
+            if b == X_READY:
                 quantise_x(x_grouped)
+                for early in range(b - 1):
+                    multiply(early)
             add_last(b)
-            if b > 0:
+            if b >= X_READY:
                 multiply(b - 1)
             if b % GROUP == 2 and b > GROUP:
                 finish(b // GROUP - 1)

@@ -25,6 +25,7 @@ UNIT = PASSES * RUN
 GROUP = 4
 GROUPS = UNITS // GROUP
 QUANT_IN = 4096
+GP_BLOCKS = 5
 X_READY = 4
 
 L2_AT, L0_AT, L1_AT, L_COLS = 0, 1024, 1280, 1344
@@ -47,7 +48,6 @@ def tile_klinear_kernel(tc, x, L0, R0, L1, R1, L2, R2, bias, out):
         results = pools.enter_context(tc.tile_pool(name="results", bufs=2))
         stage = pools.enter_context(tc.tile_pool(name="stage", bufs=1))
         r_psum = pools.enter_context(tc.psum_pool(name="r_psum", bufs=1))
-        xt_pool = pools.enter_context(tc.psum_pool(name="xt", bufs=1))
         acc_pool = pools.enter_context(tc.psum_pool(name="acc", bufs=2))
         pools.enter_context(tc.manual_schedule())
 
@@ -87,9 +87,9 @@ def tile_klinear_kernel(tc, x, L0, R0, L1, R1, L2, R2, bias, out):
         )
 
         l_third = keep.tile([P, L_COLS], F32)
-        r_small = keep.tile([P, R_COLS - R0_AT], BF16)
         r1_banks = [r_psum.tile([P, 2 * RUN], BF16, name="r1_bank%d" % h) for h in range(2)]
         r0_bank = r_psum.tile([P, 1024], BF16)
+        scalar_bank = r_psum.tile([P, 1024], BF16)
 
         def spread_l_cols(tag, at, width):
             bank = acc_pool.tile([P, 512], F32, name=tag)
@@ -110,12 +110,13 @@ def tile_klinear_kernel(tc, x, L0, R0, L1, R1, L2, R2, bias, out):
 
         bank0 = spread_l_cols("acc0", 0, 512)
         bank1 = spread_l_cols("acc1", 512, 512)
-        spread_r_rows(r0_bank[:, 512:640], R2_AT, 32)
+        spread_r_rows(scalar_bank[:, 512:640], R2_AT, 32)
+        for h in range(2):
+            spread_r_rows(scalar_bank[:, 256 * h : 256 * (h + 1)], R0_AT + 256 * h, 64)
         third_on_scalar(bank0, 0, 512)
         for h in range(2):
             spread_r_rows(r0_bank[:, 256 * h : 256 * (h + 1)], R0_AT + 256 * h, 64)
         nc.vector.tensor_scalar_mul(out=l_third[:, 512:1024], in0=bank1[:], scalar1=1.0 / 3.0)
-        nc.vector.tensor_copy(out=r_small[:], in_=r0_bank[:, 0:640])
         bank2 = spread_l_cols("acc0", L0_AT, L_COLS - L0_AT)
         nc.vector.tensor_scalar_mul(out=l_third[:, L0_AT:L_COLS], in0=bank2[:, : L_COLS - L0_AT], scalar1=1.0 / 3.0)
         for h in range(4):
@@ -136,7 +137,7 @@ def tile_klinear_kernel(tc, x, L0, R0, L1, R1, L2, R2, bias, out):
         def turn_x():
             x_grouped = stage.tile([P, PASSES, TOKENS * PACK], BF16, align_bytes=64, tag="x_a")
             for c in range(PASSES):
-                x_t = xt_pool.tile([P, 2, TOKENS], F32)
+                x_t = acc_pool.tile([P, 2, TOKENS], F32, name="acc%d" % (c % 2))
                 for u in range(2):
                     for m in range(TOKEN_TILES):
                         nc.tensor.transpose(
@@ -167,12 +168,12 @@ def tile_klinear_kernel(tc, x, L0, R0, L1, R1, L2, R2, bias, out):
         def block_of(tile_ap, j):
             return tile_ap.rearrange("p (a h f j) -> p a h f j", h=2, f=2, j=256)[:, j // 2, :, j % 2, :]
 
-        r0_row = r_small[:, 0:512].rearrange("p (h j) -> p h j", h=2)
+        r0_row = scalar_bank[:, 0:512].rearrange("p (h j) -> p h j", h=2)
         r0_psum_row = r0_bank[:, 0:512].rearrange("p (h j) -> p h j", h=2)
         partial_of, product_of, w_of, code_of, accs = {}, {}, {}, {}, {}
 
         def gp_blocks(b):
-            return 0 if b < 2 else 4 + b % 2
+            return 0 if b < 2 else GP_BLOCKS
 
         def product_cols(product, j):
             if j < 4:
@@ -186,7 +187,7 @@ def tile_klinear_kernel(tc, x, L0, R0, L1, R1, L2, R2, bias, out):
                     at = c * RUN + fg * 128
                     nc.scalar.activation(
                         out=partial[:, at : at + 128],
-                        in_=r_small[:, 512:640],
+                        in_=scalar_bank[:, 512:640],
                         func=COPY,
                         scale=l_scalar(L2_AT + c * 128 + 4 * b + fg),
                     )
@@ -203,10 +204,9 @@ def tile_klinear_kernel(tc, x, L0, R0, L1, R1, L2, R2, bias, out):
             partial, product = partial_of[b], product_of[b]
             half = slice(0, UNIT // 2)
             nc.gpsimd.tensor_tensor(out=partial[:, half], in0=partial[:, half], in1=product[:, half], op=ADD)
-            if gp_blocks(b) > 4:
-                nc.gpsimd.tensor_tensor(
-                    out=block_of(partial[:], 4), in0=block_of(partial[:], 4), in1=product_cols(product, 4), op=ADD
-                )
+            nc.gpsimd.tensor_tensor(
+                out=block_of(partial[:], 4), in0=block_of(partial[:], 4), in1=product_cols(product, 4), op=ADD
+            )
 
         def vector_sums(b):
             partial = partial_of[b]

@@ -25,7 +25,8 @@ UNIT = PASSES * RUN
 GROUP = 4
 GROUPS = UNITS // GROUP
 QUANT_IN = 4096
-GP_BLOCKS = 5
+GP_PASSES = 5
+GP_COLS = GP_PASSES * RUN
 X_READY = 4
 
 L2_AT, L0_AT, L1_AT, L_COLS = 0, 1024, 1280, 1344
@@ -43,7 +44,7 @@ def tile_klinear_kernel(tc, x, L0, R0, L1, R1, L2, R2, bias, out):
         keep = pools.enter_context(tc.tile_pool(name="keep", bufs=1))
         partials = pools.enter_context(tc.tile_pool(name="partials", bufs=4))
         products = pools.enter_context(tc.tile_pool(name="products", bufs=3))
-        blocks = pools.enter_context(tc.tile_pool(name="blocks", bufs=3))
+        blocks = pools.enter_context(tc.tile_pool(name="blocks", bufs=1))
         coded = pools.enter_context(tc.tile_pool(name="coded", bufs=6))
         results = pools.enter_context(tc.tile_pool(name="results", bufs=2))
         stage = pools.enter_context(tc.tile_pool(name="stage", bufs=1))
@@ -162,23 +163,30 @@ def tile_klinear_kernel(tc, x, L0, R0, L1, R1, L2, R2, bias, out):
         def l_scalar(at):
             return l_third[:, at : at + 1]
 
-        def l0_scalar(b, j):
-            return l_scalar(L0_AT + (j // 2) * 64 + 2 * b + j % 2)
+        def l0_scalar(b, c2, f):
+            return l_scalar(L0_AT + c2 * 64 + 2 * b + f)
 
-        def block_of(tile_ap, j):
-            return tile_ap.rearrange("p (a h f j) -> p a h f j", h=2, f=2, j=256)[:, j // 2, :, j % 2, :]
+        def runs(first, end):
+            found, c = [], first
+            while c < end:
+                size = 2 if c % 2 == 0 and c + 1 < end else 1
+                found.append((c, size))
+                c += size
+            return found
 
-        r0_row = scalar_bank[:, 0:512].rearrange("p (h j) -> p h j", h=2)
-        r0_psum_row = r0_bank[:, 0:512].rearrange("p (h j) -> p h j", h=2)
-        partial_of, product_of, w_of, code_of, accs = {}, {}, {}, {}, {}
+        def run_of(unit_ap, c, size, f):
+            return unit_ap[:, c * RUN : (c + size) * RUN].rearrange("p (c f j) -> p c f j", f=2, j=256)[:, :, f, :]
 
-        def gp_blocks(b):
-            return 0 if b < 2 else GP_BLOCKS
+        def r0_run(bank, c, size):
+            return bank[:, (c % 2) * 256 : (c % 2 + size) * 256].rearrange("p (c j) -> p c j", c=size)
 
-        def product_cols(product, j):
-            if j < 4:
-                return block_of(product[:, 0 : UNIT // 2], j)
-            return product[:, UNIT // 2 :].rearrange("p (h j) -> p h j", h=2)
+        partial_of, product_of, sum_of, w_of, code_of, accs = {}, {}, {}, {}, {}, {}
+
+        def gp_passes(b):
+            return 0 if b < 2 else GP_PASSES
+
+        def slot(b):
+            return "slot%d" % (b % 3)
 
         def scalar_products(b):
             partial = partials.tile([P, UNIT], F32)
@@ -192,44 +200,49 @@ def tile_klinear_kernel(tc, x, L0, R0, L1, R1, L2, R2, bias, out):
                         scale=l_scalar(L2_AT + c * 128 + 4 * b + fg),
                     )
             partial_of[b] = partial
-            if gp_blocks(b):
-                product = products.tile([P, UNIT // 2 + 512], F32)
-                for j in range(gp_blocks(b)):
-                    nc.scalar.activation(out=product_cols(product, j), in_=r0_row, func=COPY, scale=l0_scalar(b, j))
+            if gp_passes(b):
+                product = products.tile([P, GP_COLS], F32)
+                for c, size in runs(0, gp_passes(b)):
+                    for f in range(2):
+                        nc.scalar.activation(
+                            out=run_of(product[:], c, size, f),
+                            in_=r0_run(scalar_bank, c, size),
+                            func=COPY,
+                            scale=l0_scalar(b, c // 2, f),
+                        )
                 product_of[b] = product
 
         def gpsimd_sums(b):
-            if not gp_blocks(b):
-                return
-            partial, product = partial_of[b], product_of[b]
-            half = slice(0, UNIT // 2)
-            nc.gpsimd.tensor_tensor(out=partial[:, half], in0=partial[:, half], in1=product[:, half], op=ADD)
-            nc.gpsimd.tensor_tensor(
-                out=block_of(partial[:], 4), in0=block_of(partial[:], 4), in1=product_cols(product, 4), op=ADD
-            )
+            if gp_passes(b):
+                sums = blocks.tile([P, GP_COLS], F32, align_bytes=64, tag=slot(b - 2))
+                nc.gpsimd.tensor_tensor(out=sums[:], in0=partial_of[b][:, :GP_COLS], in1=product_of[b][:], op=ADD)
+                sum_of[b] = sums
 
         def vector_sums(b):
             partial = partial_of[b]
-            for j in range(gp_blocks(b), 8):
-                nc.vector.scalar_tensor_tensor(
-                    out=block_of(partial[:], j),
-                    in0=r0_psum_row,
-                    scalar=l0_scalar(b, j),
-                    in1=block_of(partial[:], j),
-                    op0=MULT,
-                    op1=ADD,
-                )
+            for c, size in runs(gp_passes(b), PASSES):
+                for f in range(2):
+                    nc.vector.scalar_tensor_tensor(
+                        out=run_of(partial[:], c, size, f),
+                        in0=r0_run(r0_bank, c, size),
+                        scalar=l0_scalar(b, c // 2, f),
+                        in1=run_of(partial[:], c, size, f),
+                        op0=MULT,
+                        op1=ADD,
+                    )
 
         def add_last(b):
-            w_bf16 = blocks.tile([P, UNIT], BF16, align_bytes=64)
-            for c_hi in range(2):
-                for h in range(2):
-                    cols = slice((2 * c_hi + h) * 2 * RUN, (2 * c_hi + h + 1) * 2 * RUN)
+            w_bf16 = blocks.tile([P, UNIT], BF16, align_bytes=64, tag=slot(b))
+            for c0 in range(0, PASSES, 2):
+                cuts = sorted({c0, c0 + 2, min(max(gp_passes(b), c0), c0 + 2)})
+                for c, end in zip(cuts, cuts[1:]):
+                    first_sum = sum_of[b] if c < gp_passes(b) else partial_of[b]
+                    cols = slice(c * RUN, end * RUN)
                     nc.vector.scalar_tensor_tensor(
                         out=w_bf16[:, cols],
-                        in0=r1_banks[h][:],
-                        scalar=l_scalar(L1_AT + c_hi * 32 + b),
-                        in1=partial_of[b][:, cols],
+                        in0=r1_banks[c0 // 2 % 2][:, (c - c0) * RUN : (end - c0) * RUN],
+                        scalar=l_scalar(L1_AT + c0 // 4 * 32 + b),
+                        in1=first_sum[:, cols],
                         op0=MULT,
                         op1=ADD,
                     )
@@ -267,11 +280,6 @@ def tile_klinear_kernel(tc, x, L0, R0, L1, R1, L2, R2, bias, out):
                 nc.vector.tensor_tensor(out=result[:], in0=accs[q][m][:], in1=bias_all[:, cols], op=ADD)
                 nc.sync.dma_start(out=out_rows[m * P : (m + 1) * P, cols], in_=result[:])
 
-        turnstile = keep.tile([P, 1], U32)
-
-        def gpsimd_after_quantise(b):
-            nc.gpsimd.tensor_copy(out=turnstile[:], in_=code_of[b][0][:, 0:1])
-
         order_x()
         scalar_products(0)
         scalar_products(1)
@@ -283,7 +291,6 @@ def tile_klinear_kernel(tc, x, L0, R0, L1, R1, L2, R2, bias, out):
             vector_sums(b)
             if b > 0:
                 quantise(b - 1)
-                gpsimd_after_quantise(b - 1)
             if b + 1 < UNITS:
                 gpsimd_sums(b + 1)
             if b == X_READY:

@@ -27,6 +27,7 @@ GROUPS = UNITS // GROUP
 QUANT_IN = 4096
 GP_PASSES = 5
 GP_COLS = GP_PASSES * RUN
+GP_PRODUCT = (0, 0)
 X_READY = 4
 
 L2_AT, L0_AT, L1_AT, L_COLS = 0, 1024, 1280, 1344
@@ -55,19 +56,19 @@ def tile_klinear_kernel(tc, x, L0, R0, L1, R1, L2, R2, bias, out):
         l_raw = stage.tile([P, L_COLS], BF16)
         r_raw = stage.tile([P, R_COLS], BF16)
         ident = keep.tile([P, P], F32)
-        nc.vector.memset(l_raw[:, 0:L0_AT].bitcast(U32), 0)
-        nc.vector.memset(r_raw[:, R0_AT:].bitcast(U32), 0)
         nc.vector.memset(l_raw[:, L0_AT:].bitcast(U32), 0)
+        nc.vector.memset(r_raw[:, R0_AT:].bitcast(U32), 0)
+        nc.vector.memset(l_raw[:, :L0_AT].bitcast(U32), 0)
+        nc.vector.memset(r_raw[:, :R0_AT].bitcast(U32), 0)
         make_identity(nc, ident[:])
-        nc.gpsimd.memset(r_raw[:, :R0_AT].bitcast(U32), 0)
-        nc.sync.dma_start(out=l_raw[0:16, L2_AT:L0_AT], in_=L2.rearrange("(g c) n -> g (c n)", c=8))
-        nc.sync.dma_start(out=r_raw[0:8, R2_AT:R_COLS], in_=R2.rearrange("(i t) n -> i (t n)", t=PACK))
+        nc.sync.dma_start(out=l_raw[0:16, L0_AT:L1_AT], in_=L0.rearrange("(g c) n -> g (c n)", c=4))
+        nc.sync.dma_start(out=l_raw[0:16, L1_AT:L_COLS], in_=L1.rearrange("(g c) n -> g (c n)", c=2))
         nc.sync.dma_start(
             out=r_raw[0:8, R0_AT:R2_AT].rearrange("p (c j) -> p c j", c=2),
             in_=R0.rearrange("(c i t) n -> i c (t n)", c=2, t=PACK),
         )
-        nc.sync.dma_start(out=l_raw[0:16, L0_AT:L1_AT], in_=L0.rearrange("(g c) n -> g (c n)", c=4))
-        nc.sync.dma_start(out=l_raw[0:16, L1_AT:L_COLS], in_=L1.rearrange("(g c) n -> g (c n)", c=2))
+        nc.sync.dma_start(out=r_raw[0:8, R2_AT:R_COLS], in_=R2.rearrange("(i t) n -> i (t n)", t=PACK))
+        nc.sync.dma_start(out=l_raw[0:16, L2_AT:L0_AT], in_=L2.rearrange("(g c) n -> g (c n)", c=8))
         nc.sync.dma_start(
             out=r_raw[0:8, R1_AT:R0_AT].rearrange("p (c j) -> p c j", c=4),
             in_=R1.rearrange("(c i t) n -> i c (t n)", c=4, t=PACK),
@@ -89,16 +90,13 @@ def tile_klinear_kernel(tc, x, L0, R0, L1, R1, L2, R2, bias, out):
 
         l_third = keep.tile([P, L_COLS], F32)
         r1_banks = [r_psum.tile([P, 2 * RUN], BF16, name="r1_bank%d" % h) for h in range(2)]
-        r0_bank = r_psum.tile([P, 1024], BF16)
-        scalar_bank = r_psum.tile([P, 1024], BF16)
+        r02_bank = r_psum.tile([P, 1024], BF16)
+        r02_sbuf = keep.tile([P, RUN + 128], BF16)
 
         def spread_l_cols(tag, at, width):
             bank = acc_pool.tile([P, 512], F32, name=tag)
             nc.tensor.matmul(out=bank[:, :width], lhsT=spread_l[:], rhs=l_raw[:, at : at + width], start=True, stop=True)
             return bank
-
-        def third_on_scalar(bank, at, width):
-            nc.scalar.activation(out=l_third[:, at : at + width], in_=bank[:, :width], func=COPY, scale=1.0 / 3.0)
 
         def spread_r_rows(bank_cols, at, cols):
             nc.tensor.matmul(
@@ -109,23 +107,21 @@ def tile_klinear_kernel(tc, x, L0, R0, L1, R1, L2, R2, bias, out):
                 stop=True,
             )
 
-        bank0 = spread_l_cols("acc0", 0, 512)
-        bank1 = spread_l_cols("acc1", 512, 512)
-        spread_r_rows(scalar_bank[:, 512:640], R2_AT, 32)
+        bank = spread_l_cols("acc0", L0_AT, L_COLS - L0_AT)
+        nc.vector.tensor_scalar_mul(out=l_third[:, L0_AT:], in0=bank[:, : L_COLS - L0_AT], scalar1=1.0 / 3.0)
         for h in range(2):
-            spread_r_rows(scalar_bank[:, 256 * h : 256 * (h + 1)], R0_AT + 256 * h, 64)
-        third_on_scalar(bank0, 0, 512)
+            spread_r_rows(r02_bank[:, 256 * h : 256 * (h + 1)], R0_AT + 256 * h, 64)
+        spread_r_rows(r02_bank[:, RUN : RUN + 128], R2_AT, 32)
+        nc.vector.tensor_copy(out=r02_sbuf[:], in_=r02_bank[:, : RUN + 128])
         for h in range(2):
-            spread_r_rows(r0_bank[:, 256 * h : 256 * (h + 1)], R0_AT + 256 * h, 64)
-        nc.vector.tensor_scalar_mul(out=l_third[:, 512:1024], in0=bank1[:], scalar1=1.0 / 3.0)
-        bank2 = spread_l_cols("acc0", L0_AT, L_COLS - L0_AT)
-        nc.vector.tensor_scalar_mul(out=l_third[:, L0_AT:L_COLS], in0=bank2[:, : L_COLS - L0_AT], scalar1=1.0 / 3.0)
+            bank = spread_l_cols("acc%d" % (1 - h), 512 * h, 512)
+            nc.scalar.activation(out=l_third[:, 512 * h : 512 * (h + 1)], in_=bank[:], func=COPY, scale=1.0 / 3.0)
         for h in range(4):
             spread_r_rows(r1_banks[h // 2][:, RUN * (h % 2) : RUN * (h % 2 + 1)], R1_AT + RUN * h, UNIT_COLS)
 
         x_codes = keep.tile([P, PASSES * TOKENS], U32, align_bytes=64)
         x_scales = keep.tile([P, PASSES * TOKENS], U8, align_bytes=64)
-        x_words = stage.tile([P, TOKEN_TILES, 2, D // 4], F32)
+        x_words = partials.tile([P, TOKEN_TILES, 2, D // 4], F32, tag="partial")
 
         def order_x():
             for m in range(TOKEN_TILES):
@@ -188,6 +184,26 @@ def tile_klinear_kernel(tc, x, L0, R0, L1, R1, L2, R2, bias, out):
         def slot(b):
             return "slot%d" % (b % 3)
 
+        def first_unit():
+            partial = partials.tile([P, UNIT], F32)
+            partial_of[0] = partial
+            for c in range(0, PASSES, 2):
+                for f in range(2):
+                    nc.vector.tensor_scalar_mul(
+                        out=run_of(partial[:], c, 2, f), in0=r0_run(r02_sbuf, c, 2), scalar1=l0_scalar(0, c // 2, f)
+                    )
+            for c in range(PASSES):
+                for fg in range(4):
+                    cols = slice(c * RUN + fg * 128, c * RUN + (fg + 1) * 128)
+                    nc.vector.scalar_tensor_tensor(
+                        out=partial[:, cols],
+                        in0=r02_bank[:, RUN : RUN + 128],
+                        scalar=l_scalar(L2_AT + c * 128 + fg),
+                        in1=partial[:, cols],
+                        op0=MULT,
+                        op1=ADD,
+                    )
+
         def scalar_products(b):
             partial = partials.tile([P, UNIT], F32)
             for c in range(PASSES):
@@ -195,25 +211,35 @@ def tile_klinear_kernel(tc, x, L0, R0, L1, R1, L2, R2, bias, out):
                     at = c * RUN + fg * 128
                     nc.scalar.activation(
                         out=partial[:, at : at + 128],
-                        in_=scalar_bank[:, 512:640],
+                        in_=r02_sbuf[:, RUN:],
                         func=COPY,
                         scale=l_scalar(L2_AT + c * 128 + 4 * b + fg),
                     )
             partial_of[b] = partial
             if gp_passes(b):
                 product = products.tile([P, GP_COLS], F32)
+                product_of[b] = product
                 for c, size in runs(0, gp_passes(b)):
                     for f in range(2):
-                        nc.scalar.activation(
-                            out=run_of(product[:], c, size, f),
-                            in_=r0_run(scalar_bank, c, size),
-                            func=COPY,
-                            scale=l0_scalar(b, c // 2, f),
-                        )
-                product_of[b] = product
+                        if (c, f) != GP_PRODUCT:
+                            nc.scalar.activation(
+                                out=run_of(product[:], c, size, f),
+                                in_=r0_run(r02_sbuf, c, size),
+                                func=COPY,
+                                scale=l0_scalar(b, c // 2, f),
+                            )
 
         def gpsimd_sums(b):
             if gp_passes(b):
+                c, f = GP_PRODUCT
+                nc.gpsimd.tensor_scalar(
+                    out=run_of(product_of[b][:], c, 2, f),
+                    in0=r0_run(r02_sbuf, c, 2),
+                    scalar1=l0_scalar(b, c // 2, f),
+                    scalar2=0.0,
+                    op0=MULT,
+                    op1=ADD,
+                )
                 sums = blocks.tile([P, GP_COLS], F32, align_bytes=64, tag=slot(b - 2))
                 nc.gpsimd.tensor_tensor(out=sums[:], in0=partial_of[b][:, :GP_COLS], in1=product_of[b][:], op=ADD)
                 sum_of[b] = sums
@@ -224,7 +250,7 @@ def tile_klinear_kernel(tc, x, L0, R0, L1, R1, L2, R2, bias, out):
                 for f in range(2):
                     nc.vector.scalar_tensor_tensor(
                         out=run_of(partial[:], c, size, f),
-                        in0=r0_run(r0_bank, c, size),
+                        in0=r0_run(r02_bank, c, size),
                         scalar=l0_scalar(b, c // 2, f),
                         in1=run_of(partial[:], c, size, f),
                         op0=MULT,
@@ -280,15 +306,16 @@ def tile_klinear_kernel(tc, x, L0, R0, L1, R1, L2, R2, bias, out):
                 nc.vector.tensor_tensor(out=result[:], in0=accs[q][m][:], in1=bias_all[:, cols], op=ADD)
                 nc.sync.dma_start(out=out_rows[m * P : (m + 1) * P, cols], in_=result[:])
 
+        first_unit()
         order_x()
-        scalar_products(0)
         scalar_products(1)
         for b in range(UNITS):
-            if b + 2 < UNITS:
-                scalar_products(b + 2)
             if b == 1:
                 x_grouped = turn_x()
-            vector_sums(b)
+            if b + 2 < UNITS:
+                scalar_products(b + 2)
+            if b > 0:
+                vector_sums(b)
             if b > 0:
                 quantise(b - 1)
             if b + 1 < UNITS:

@@ -27,6 +27,7 @@ GROUPS = UNITS // GROUP
 QUANT_IN = 4096
 GP_PASSES = 5
 GP_COLS = GP_PASSES * RUN
+SUM_PASSES = 6
 GP_PRODUCT = (0, 0)
 X_READY = 4
 
@@ -121,15 +122,18 @@ def tile_klinear_kernel(tc, x, L0, R0, L1, R1, L2, R2, bias, out):
 
         x_codes = keep.tile([P, PASSES * TOKENS], U32, align_bytes=64)
         x_scales = keep.tile([P, PASSES * TOKENS], U8, align_bytes=64)
-        x_words = partials.tile([P, TOKEN_TILES, 2, D // 4], F32, tag="partial")
+        x_words = stage.tile([P, TOKEN_TILES, 2, D // 4], U32)
 
         def order_x():
             for m in range(TOKEN_TILES):
-                by_u = x_sb[:, m, :].bitcast(F32).rearrange("p (g c i u) -> p u c g i", c=8, i=8, u=2)
+                by_u = x_sb[:, m, :].bitcast(U32).rearrange("p (g c i u) -> p u c g i", c=8, i=8, u=2)
                 for u in range(2):
-                    nc.vector.tensor_copy(
-                        out=x_words[:, m, u, :].rearrange("p (c g i) -> p c g i", c=8, i=8), in_=by_u[:, u]
-                    )
+                    for half in range(2):
+                        part = slice(half * 4, half * 4 + 4)
+                        nc.gpsimd.tensor_copy(
+                            out=x_words[:, m, u, :].rearrange("p (c g i) -> p c g i", c=8, i=8)[:, part],
+                            in_=by_u[:, u, part],
+                        )
 
         def turn_x():
             x_grouped = stage.tile([P, PASSES, TOKENS * PACK], BF16, align_bytes=64, tag="x_a")
@@ -138,7 +142,7 @@ def tile_klinear_kernel(tc, x, L0, R0, L1, R1, L2, R2, bias, out):
                 for u in range(2):
                     for m in range(TOKEN_TILES):
                         nc.tensor.transpose(
-                            x_t[:, u, m * P : (m + 1) * P], x_words[:, m, u, c * P : (c + 1) * P], ident[:]
+                            x_t[:, u, m * P : (m + 1) * P], x_words[:, m, u, c * P : (c + 1) * P].bitcast(F32), ident[:]
                         )
                 nc.scalar.copy(
                     out=x_grouped[:, c, :].bitcast(F32).rearrange("p (r u) -> p r u", u=2),
@@ -177,6 +181,9 @@ def tile_klinear_kernel(tc, x, L0, R0, L1, R1, L2, R2, bias, out):
             return bank[:, (c % 2) * 256 : (c % 2 + size) * 256].rearrange("p (c j) -> p c j", c=size)
 
         partial_of, product_of, sum_of, w_of, code_of, accs = {}, {}, {}, {}, {}, {}
+
+        def gpsimd_product(b):
+            return b % 2 == 1
 
         def gp_passes(b):
             return 0 if b < 2 else GP_PASSES
@@ -221,7 +228,7 @@ def tile_klinear_kernel(tc, x, L0, R0, L1, R1, L2, R2, bias, out):
                 product_of[b] = product
                 for c, size in runs(0, gp_passes(b)):
                     for f in range(2):
-                        if (c, f) != GP_PRODUCT:
+                        if not (gpsimd_product(b) and (c, f) == GP_PRODUCT):
                             nc.scalar.activation(
                                 out=run_of(product[:], c, size, f),
                                 in_=r0_run(r02_sbuf, c, size),
@@ -231,25 +238,31 @@ def tile_klinear_kernel(tc, x, L0, R0, L1, R1, L2, R2, bias, out):
 
         def gpsimd_sums(b):
             if gp_passes(b):
-                c, f = GP_PRODUCT
-                nc.gpsimd.tensor_scalar(
-                    out=run_of(product_of[b][:], c, 2, f),
-                    in0=r0_run(r02_sbuf, c, 2),
-                    scalar1=l0_scalar(b, c // 2, f),
-                    scalar2=0.0,
-                    op0=MULT,
-                    op1=ADD,
+                if gpsimd_product(b):
+                    c, f = GP_PRODUCT
+                    nc.gpsimd.tensor_scalar(
+                        out=run_of(product_of[b][:], c, 2, f),
+                        in0=r0_run(r02_sbuf, c, 2),
+                        scalar1=l0_scalar(b, c // 2, f),
+                        scalar2=0.0,
+                        op0=MULT,
+                        op1=ADD,
+                    )
+                sums = blocks.tile([P, SUM_PASSES * RUN], F32, align_bytes=64, tag=slot(b - 2))
+                nc.gpsimd.tensor_tensor(
+                    out=sums[:, :GP_COLS], in0=partial_of[b][:, :GP_COLS], in1=product_of[b][:], op=ADD
                 )
-                sums = blocks.tile([P, GP_COLS], F32, align_bytes=64, tag=slot(b - 2))
-                nc.gpsimd.tensor_tensor(out=sums[:], in0=partial_of[b][:, :GP_COLS], in1=product_of[b][:], op=ADD)
                 sum_of[b] = sums
+
+        def first_sum_of(b, c):
+            return sum_of[b] if gp_passes(b) and c < SUM_PASSES else partial_of[b]
 
         def vector_sums(b):
             partial = partial_of[b]
             for c, size in runs(gp_passes(b), PASSES):
                 for f in range(2):
                     nc.vector.scalar_tensor_tensor(
-                        out=run_of(partial[:], c, size, f),
+                        out=run_of(first_sum_of(b, c)[:], c, size, f),
                         in0=r0_run(r02_bank, c, size),
                         scalar=l0_scalar(b, c // 2, f),
                         in1=run_of(partial[:], c, size, f),
@@ -257,36 +270,38 @@ def tile_klinear_kernel(tc, x, L0, R0, L1, R1, L2, R2, bias, out):
                         op1=ADD,
                     )
 
-        def add_last(b):
-            w_bf16 = blocks.tile([P, UNIT], BF16, align_bytes=64, tag=slot(b))
-            for c0 in range(0, PASSES, 2):
-                cuts = sorted({c0, c0 + 2, min(max(gp_passes(b), c0), c0 + 2)})
-                for c, end in zip(cuts, cuts[1:]):
-                    first_sum = sum_of[b] if c < gp_passes(b) else partial_of[b]
-                    cols = slice(c * RUN, end * RUN)
-                    nc.vector.scalar_tensor_tensor(
-                        out=w_bf16[:, cols],
-                        in0=r1_banks[c0 // 2 % 2][:, (c - c0) * RUN : (end - c0) * RUN],
-                        scalar=l_scalar(L1_AT + c0 // 4 * 32 + b),
-                        in1=first_sum[:, cols],
-                        op0=MULT,
-                        op1=ADD,
-                    )
-            w_of[b] = w_bf16
+        def add_last(b, chunks=range(0, PASSES, 2)):
+            if b not in w_of:
+                w_of[b] = blocks.tile([P, UNIT], BF16, align_bytes=64, tag=slot(b), name="w_bf16")
+            for c in chunks:
+                cols = slice(c * RUN, (c + 2) * RUN)
+                nc.vector.scalar_tensor_tensor(
+                    out=w_of[b][:, cols],
+                    in0=r1_banks[c // 2 % 2][:],
+                    scalar=l_scalar(L1_AT + c // 4 * 32 + b),
+                    in1=first_sum_of(b, c)[:, cols],
+                    op0=MULT,
+                    op1=ADD,
+                )
 
-        def quantise(b):
-            w_codes = coded.tile([P, PASSES * UNIT_COLS], U32, align_bytes=64)
-            w_scales = coded.tile([P, PASSES * UNIT_COLS], U8, align_bytes=64)
-            nc.vector.quantize_mx(out=w_codes[:].bitcast(FP8X4), scales=w_scales[:], in_=w_of[b][:])
-            code_of[b] = (w_codes, w_scales)
+        def quantise(b, first=0, end=PASSES):
+            if b not in code_of:
+                w_codes = coded.tile([P, PASSES * UNIT_COLS], U32, align_bytes=64)
+                w_scales = coded.tile([P, PASSES * UNIT_COLS], U8, align_bytes=64)
+                code_of[b] = (w_codes, w_scales)
+            w_codes, w_scales = code_of[b]
+            words = slice(first * UNIT_COLS, end * UNIT_COLS)
+            nc.vector.quantize_mx(
+                out=w_codes[:, words].bitcast(FP8X4), scales=w_scales[:, words], in_=w_of[b][:, first * RUN : end * RUN]
+            )
 
-        def multiply(b):
-            if b % GROUP == 0:
+        def multiply(b, first=0, end=PASSES):
+            if b // GROUP not in accs:
                 accs[b // GROUP] = [acc_pool.tile([P, GROUP * UNIT_COLS], F32, name="acc%d" % m) for m in range(2)]
             acc = accs[b // GROUP]
             w_codes, w_scales = code_of[b]
             for m in range(TOKEN_TILES):
-                for c in range(PASSES):
+                for c in range(first, end):
                     x_cols = slice(c * TOKENS + m * P, c * TOKENS + (m + 1) * P)
                     w_cols = slice(c * UNIT_COLS, (c + 1) * UNIT_COLS)
                     nc.tensor.matmul_mx(
@@ -299,21 +314,25 @@ def tile_klinear_kernel(tc, x, L0, R0, L1, R1, L2, R2, bias, out):
                         stop=(c == PASSES - 1),
                     )
 
-        def finish(q):
-            cols = slice(q * GROUP * UNIT_COLS, (q + 1) * GROUP * UNIT_COLS)
+        def finish(first, end):
+            q = first // GROUP
+            bank_cols = slice((first % GROUP) * UNIT_COLS, (first % GROUP + end - first) * UNIT_COLS)
+            cols = slice(first * UNIT_COLS, end * UNIT_COLS)
             for m in range(TOKEN_TILES):
                 result = results.tile([P, GROUP * UNIT_COLS], F32, name="result%d" % m)
-                nc.vector.tensor_tensor(out=result[:], in0=accs[q][m][:], in1=bias_all[:, cols], op=ADD)
-                nc.sync.dma_start(out=out_rows[m * P : (m + 1) * P, cols], in_=result[:])
+                nc.vector.tensor_tensor(
+                    out=result[:, bank_cols], in0=accs[q][m][:, bank_cols], in1=bias_all[:, cols], op=ADD
+                )
+                nc.sync.dma_start(out=out_rows[m * P : (m + 1) * P, cols], in_=result[:, bank_cols])
 
         first_unit()
         order_x()
         scalar_products(1)
         for b in range(UNITS):
-            if b == 1:
-                x_grouped = turn_x()
             if b + 2 < UNITS:
                 scalar_products(b + 2)
+            if b == 1:
+                x_grouped = turn_x()
             if b > 0:
                 vector_sums(b)
             if b > 0:
@@ -324,11 +343,21 @@ def tile_klinear_kernel(tc, x, L0, R0, L1, R1, L2, R2, bias, out):
                 quantise_x(x_grouped)
                 for early in range(b - 1):
                     multiply(early)
+            if b == UNITS - 1:
+                break
             add_last(b)
             if b >= X_READY:
                 multiply(b - 1)
             if b % GROUP == 2 and b > GROUP:
-                finish(b // GROUP - 1)
-        quantise(UNITS - 1)
-        multiply(UNITS - 1)
-        finish(GROUPS - 1)
+                finish(b - 2 - GROUP, b - 2)
+
+        last = UNITS - 1
+        multiply(last - 1)
+        add_last(last, (0, 2, 4))
+        finish(last - GROUP + 1, last)
+        quantise(last, 0, PASSES // 2)
+        multiply(last, 0, PASSES // 2)
+        add_last(last, (6,))
+        quantise(last, PASSES // 2)
+        multiply(last, PASSES // 2)
+        finish(last, UNITS)

from contextlib import ExitStack

import concourse.mybir as mybir
from concourse.masks import make_identity

F32 = mybir.dt.float32
BF16 = mybir.dt.bfloat16
U32 = mybir.dt.uint32
U8 = mybir.dt.uint8
FP8X4 = mybir.dt.float8_e4m3fn_x4
MULT = mybir.AluOpType.mult
ADD = mybir.AluOpType.add
COPY = mybir.ActivationFunctionType.Copy

P = 128
D = 4096
TOKENS = 256
TOKEN_TILES = TOKENS // P
PACK = 4
PASSES = D // (P * PACK)
UNITS = 32
UNIT_COLS = D // UNITS
RUN = UNIT_COLS * PACK
UNIT = PASSES * RUN
GROUP = 4
GROUPS = UNITS // GROUP
QUANT_IN = 4096
GP_PASSES = 5
GP_COLS = GP_PASSES * RUN
SUM_PASSES = 6
GP_PRODUCT = (0, 0)
X_READY = 4

L2_AT, L0_AT, L1_AT, L_COLS = 0, 1024, 1280, 1344
R1_AT, R0_AT, R2_AT, R_COLS = 0, 2048, 2560, 2688

FLOPS = 2 * TOKENS * D * D


def tile_klinear_kernel(tc, x, L0, R0, L1, R1, L2, R2, bias, out):
    nc = tc.nc
    x_rows = x.flatten_outer_dims()
    out_rows = out.flatten_outer_dims()

    with ExitStack() as pools:
        keep = pools.enter_context(tc.tile_pool(name="keep", bufs=1))
        partials = pools.enter_context(tc.tile_pool(name="partials", bufs=4))
        products = pools.enter_context(tc.tile_pool(name="products", bufs=3))
        blocks = pools.enter_context(tc.tile_pool(name="blocks", bufs=1))
        coded = pools.enter_context(tc.tile_pool(name="coded", bufs=6))
        results = pools.enter_context(tc.tile_pool(name="results", bufs=2))
        stage = pools.enter_context(tc.tile_pool(name="stage", bufs=1))
        r_psum = pools.enter_context(tc.psum_pool(name="r_psum", bufs=1))
        acc_pool = pools.enter_context(tc.psum_pool(name="acc", bufs=2))
        pools.enter_context(tc.manual_schedule())

        l_raw = stage.tile([P, L_COLS], BF16)
        r_raw = stage.tile([P, R_COLS], BF16)
        ident = keep.tile([P, P], F32)
        nc.vector.memset(l_raw[:, L0_AT:].bitcast(U32), 0)
        nc.vector.memset(r_raw[:, R0_AT:].bitcast(U32), 0)
        nc.vector.memset(l_raw[:, :L0_AT].bitcast(U32), 0)
        nc.vector.memset(r_raw[:, :R0_AT].bitcast(U32), 0)
        make_identity(nc, ident[:])
        nc.sync.dma_start(out=l_raw[0:16, L0_AT:L1_AT], in_=L0.rearrange("(g c) n -> g (c n)", c=4))
        nc.sync.dma_start(out=l_raw[0:16, L1_AT:L_COLS], in_=L1.rearrange("(g c) n -> g (c n)", c=2))
        nc.sync.dma_start(
            out=r_raw[0:8, R0_AT:R2_AT].rearrange("p (c j) -> p c j", c=2),
            in_=R0.rearrange("(c i t) n -> i c (t n)", c=2, t=PACK),
        )
        nc.sync.dma_start(out=r_raw[0:8, R2_AT:R_COLS], in_=R2.rearrange("(i t) n -> i (t n)", t=PACK))
        nc.sync.dma_start(out=l_raw[0:16, L2_AT:L0_AT], in_=L2.rearrange("(g c) n -> g (c n)", c=8))
        nc.sync.dma_start(
            out=r_raw[0:8, R1_AT:R0_AT].rearrange("p (c j) -> p c j", c=4),
            in_=R1.rearrange("(c i t) n -> i c (t n)", c=4, t=PACK),
        )
        x_sb = stage.tile([P, TOKEN_TILES, D], BF16, align_bytes=64, tag="x_a")
        for m in range(TOKEN_TILES):
            nc.sync.dma_start(out=x_sb[:, m, :], in_=x_rows[m * P : (m + 1) * P, :])
        bias_all = keep.tile([P, D], BF16)
        nc.sync.dma_start(out=bias_all[:], in_=bias.partition_broadcast(P))

        spread_l = keep.tile([P, P], BF16)
        spread_r = keep.tile([P, P], BF16)
        nc.vector.tensor_copy(
            out=spread_l[:].rearrange("k (g i) -> k g i", i=8), in_=ident[:, 0:16].unsqueeze(2).to_broadcast([P, 16, 8])
        )
        nc.vector.tensor_copy(
            out=spread_r[:].rearrange("k (g i) -> k g i", i=8), in_=ident[:, 0:8].unsqueeze(1).to_broadcast([P, 16, 8])
        )

        l_third = keep.tile([P, L_COLS], F32)
        r1_banks = [r_psum.tile([P, 2 * RUN], BF16, name="r1_bank%d" % h) for h in range(2)]
        r02_bank = r_psum.tile([P, 1024], BF16)
        r02_sbuf = keep.tile([P, RUN + 128], BF16)

        def spread_l_cols(tag, at, width):
            bank = acc_pool.tile([P, 512], F32, name=tag)
            nc.tensor.matmul(out=bank[:, :width], lhsT=spread_l[:], rhs=l_raw[:, at : at + width], start=True, stop=True)
            return bank

        def spread_r_rows(bank_cols, at, cols):
            nc.tensor.matmul(
                out=bank_cols,
                lhsT=spread_r[:],
                rhs=r_raw[:, at : at + PACK * cols].rearrange("p (t n) -> p n t", t=PACK),
                start=True,
                stop=True,
            )

        bank = spread_l_cols("acc0", L0_AT, L_COLS - L0_AT)
        nc.vector.tensor_scalar_mul(out=l_third[:, L0_AT:], in0=bank[:, : L_COLS - L0_AT], scalar1=1.0 / 3.0)
        for h in range(2):
            spread_r_rows(r02_bank[:, 256 * h : 256 * (h + 1)], R0_AT + 256 * h, 64)
        spread_r_rows(r02_bank[:, RUN : RUN + 128], R2_AT, 32)
        nc.vector.tensor_copy(out=r02_sbuf[:], in_=r02_bank[:, : RUN + 128])
        for h in range(2):
            bank = spread_l_cols("acc%d" % (1 - h), 512 * h, 512)
            nc.scalar.activation(out=l_third[:, 512 * h : 512 * (h + 1)], in_=bank[:], func=COPY, scale=1.0 / 3.0)
        for h in range(4):
            spread_r_rows(r1_banks[h // 2][:, RUN * (h % 2) : RUN * (h % 2 + 1)], R1_AT + RUN * h, UNIT_COLS)

        x_codes = keep.tile([P, PASSES * TOKENS], U32, align_bytes=64)
        x_scales = keep.tile([P, PASSES * TOKENS], U8, align_bytes=64)
        x_words = stage.tile([P, TOKEN_TILES, 2, D // 4], U32)

        def order_x():
            for m in range(TOKEN_TILES):
                by_u = x_sb[:, m, :].bitcast(U32).rearrange("p (g c i u) -> p u c g i", c=8, i=8, u=2)
                for u in range(2):
                    for half in range(2):
                        part = slice(half * 4, half * 4 + 4)
                        nc.gpsimd.tensor_copy(
                            out=x_words[:, m, u, :].rearrange("p (c g i) -> p c g i", c=8, i=8)[:, part],
                            in_=by_u[:, u, part],
                        )

        def turn_x():
            x_grouped = stage.tile([P, PASSES, TOKENS * PACK], BF16, align_bytes=64, tag="x_a")
            for c in range(PASSES):
                x_t = acc_pool.tile([P, 2, TOKENS], F32, name="acc%d" % (c % 2))
                for u in range(2):
                    for m in range(TOKEN_TILES):
                        nc.tensor.transpose(
                            x_t[:, u, m * P : (m + 1) * P], x_words[:, m, u, c * P : (c + 1) * P].bitcast(F32), ident[:]
                        )
                nc.scalar.copy(
                    out=x_grouped[:, c, :].bitcast(F32).rearrange("p (r u) -> p r u", u=2),
                    in_=x_t[:].rearrange("p u r -> p r u"),
                )
            return x_grouped

        def quantise_x(x_grouped):
            x_flat = x_grouped[:].rearrange("p c j -> p (c j)")
            for h in range(PASSES * TOKENS * PACK // QUANT_IN):
                words = slice(h * QUANT_IN // PACK, (h + 1) * QUANT_IN // PACK)
                nc.vector.quantize_mx(
                    out=x_codes[:, words].bitcast(FP8X4),
                    scales=x_scales[:, words],
                    in_=x_flat[:, h * QUANT_IN : (h + 1) * QUANT_IN],
                )

        def l_scalar(at):
            return l_third[:, at : at + 1]

        def l0_scalar(b, c2, f):
            return l_scalar(L0_AT + c2 * 64 + 2 * b + f)

        def runs(first, end):
            found, c = [], first
            while c < end:
                size = 2 if c % 2 == 0 and c + 1 < end else 1
                found.append((c, size))
                c += size
            return found

        def run_of(unit_ap, c, size, f):
            return unit_ap[:, c * RUN : (c + size) * RUN].rearrange("p (c f j) -> p c f j", f=2, j=256)[:, :, f, :]

        def r0_run(bank, c, size):
            return bank[:, (c % 2) * 256 : (c % 2 + size) * 256].rearrange("p (c j) -> p c j", c=size)

        partial_of, product_of, sum_of, w_of, code_of, accs = {}, {}, {}, {}, {}, {}

        def gpsimd_product(b):
            return b % 2 == 1

        def gp_passes(b):
            return 0 if b < 2 else GP_PASSES

        def slot(b):
            return "slot%d" % (b % 3)

        def first_unit():
            partial = partials.tile([P, UNIT], F32)
            partial_of[0] = partial
            for c in range(0, PASSES, 2):
                for f in range(2):
                    nc.vector.tensor_scalar_mul(
                        out=run_of(partial[:], c, 2, f), in0=r0_run(r02_sbuf, c, 2), scalar1=l0_scalar(0, c // 2, f)
                    )
            for c in range(PASSES):
                for fg in range(4):
                    cols = slice(c * RUN + fg * 128, c * RUN + (fg + 1) * 128)
                    nc.vector.scalar_tensor_tensor(
                        out=partial[:, cols],
                        in0=r02_bank[:, RUN : RUN + 128],
                        scalar=l_scalar(L2_AT + c * 128 + fg),
                        in1=partial[:, cols],
                        op0=MULT,
                        op1=ADD,
                    )

        def scalar_products(b):
            partial = partials.tile([P, UNIT], F32)
            for c in range(PASSES):
                for fg in range(4):
                    at = c * RUN + fg * 128
                    nc.scalar.activation(
                        out=partial[:, at : at + 128],
                        in_=r02_sbuf[:, RUN:],
                        func=COPY,
                        scale=l_scalar(L2_AT + c * 128 + 4 * b + fg),
                    )
            partial_of[b] = partial
            if gp_passes(b):
                product = products.tile([P, GP_COLS], F32)
                product_of[b] = product
                for c, size in runs(0, gp_passes(b)):
                    for f in range(2):
                        if not (gpsimd_product(b) and (c, f) == GP_PRODUCT):
                            nc.scalar.activation(
                                out=run_of(product[:], c, size, f),
                                in_=r0_run(r02_sbuf, c, size),
                                func=COPY,
                                scale=l0_scalar(b, c // 2, f),
                            )

        def gpsimd_sums(b):
            if gp_passes(b):
                if gpsimd_product(b):
                    c, f = GP_PRODUCT
                    nc.gpsimd.tensor_scalar(
                        out=run_of(product_of[b][:], c, 2, f),
                        in0=r0_run(r02_sbuf, c, 2),
                        scalar1=l0_scalar(b, c // 2, f),
                        scalar2=0.0,
                        op0=MULT,
                        op1=ADD,
                    )
                sums = blocks.tile([P, SUM_PASSES * RUN], F32, align_bytes=64, tag=slot(b - 2))
                nc.gpsimd.tensor_tensor(
                    out=sums[:, :GP_COLS], in0=partial_of[b][:, :GP_COLS], in1=product_of[b][:], op=ADD
                )
                sum_of[b] = sums

        def first_sum_of(b, c):
            return sum_of[b] if gp_passes(b) and c < SUM_PASSES else partial_of[b]

        def vector_sums(b):
            partial = partial_of[b]
            for c, size in runs(gp_passes(b), PASSES):
                for f in range(2):
                    nc.vector.scalar_tensor_tensor(
                        out=run_of(first_sum_of(b, c)[:], c, size, f),
                        in0=r0_run(r02_bank, c, size),
                        scalar=l0_scalar(b, c // 2, f),
                        in1=run_of(partial[:], c, size, f),
                        op0=MULT,
                        op1=ADD,
                    )

        def add_last(b, chunks=range(0, PASSES, 2)):
            if b not in w_of:
                w_of[b] = blocks.tile([P, UNIT], BF16, align_bytes=64, tag=slot(b), name="w_bf16")
            for c in chunks:
                cols = slice(c * RUN, (c + 2) * RUN)
                nc.vector.scalar_tensor_tensor(
                    out=w_of[b][:, cols],
                    in0=r1_banks[c // 2 % 2][:],
                    scalar=l_scalar(L1_AT + c // 4 * 32 + b),
                    in1=first_sum_of(b, c)[:, cols],
                    op0=MULT,
                    op1=ADD,
                )

        def quantise(b, first=0, end=PASSES):
            if b not in code_of:
                w_codes = coded.tile([P, PASSES * UNIT_COLS], U32, align_bytes=64)
                w_scales = coded.tile([P, PASSES * UNIT_COLS], U8, align_bytes=64)
                code_of[b] = (w_codes, w_scales)
            w_codes, w_scales = code_of[b]
            words = slice(first * UNIT_COLS, end * UNIT_COLS)
            nc.vector.quantize_mx(
                out=w_codes[:, words].bitcast(FP8X4), scales=w_scales[:, words], in_=w_of[b][:, first * RUN : end * RUN]
            )

        def multiply(b, first=0, end=PASSES):
            if b // GROUP not in accs:
                accs[b // GROUP] = [acc_pool.tile([P, GROUP * UNIT_COLS], F32, name="acc%d" % m) for m in range(2)]
            acc = accs[b // GROUP]
            w_codes, w_scales = code_of[b]
            for m in range(TOKEN_TILES):
                for c in range(first, end):
                    x_cols = slice(c * TOKENS + m * P, c * TOKENS + (m + 1) * P)
                    w_cols = slice(c * UNIT_COLS, (c + 1) * UNIT_COLS)
                    nc.tensor.matmul_mx(
                        out=acc[m][:, (b % GROUP) * UNIT_COLS : (b % GROUP + 1) * UNIT_COLS],
                        lhsT=x_codes[:, x_cols].bitcast(FP8X4),
                        lhsT_scale=x_scales[:, x_cols],
                        rhs=w_codes[:, w_cols].bitcast(FP8X4),
                        rhs_scale=w_scales[:, w_cols],
                        start=(c == 0),
                        stop=(c == PASSES - 1),
                    )

        def finish(first, end):
            q = first // GROUP
            bank_cols = slice((first % GROUP) * UNIT_COLS, (first % GROUP + end - first) * UNIT_COLS)
            cols = slice(first * UNIT_COLS, end * UNIT_COLS)
            for m in range(TOKEN_TILES):
                result = results.tile([P, GROUP * UNIT_COLS], F32, name="result%d" % m)
                nc.vector.tensor_tensor(
                    out=result[:, bank_cols], in0=accs[q][m][:, bank_cols], in1=bias_all[:, cols], op=ADD
                )
                nc.sync.dma_start(out=out_rows[m * P : (m + 1) * P, cols], in_=result[:, bank_cols])

        first_unit()
        order_x()
        scalar_products(1)
        for b in range(UNITS):
            if b + 2 < UNITS:
                scalar_products(b + 2)
            if b == 1:
                x_grouped = turn_x()
            if b > 0:
                vector_sums(b)
            if b > 0:
                quantise(b - 1)
            if b + 1 < UNITS:
                gpsimd_sums(b + 1)
            if b == X_READY:
                quantise_x(x_grouped)
                for early in range(b - 1):
                    multiply(early)
            if b == UNITS - 1:
                break
            add_last(b)
            if b >= X_READY:
                multiply(b - 1)
            if b % GROUP == 2 and b > GROUP:
                finish(b - 2 - GROUP, b - 2)

        last = UNITS - 1
        multiply(last - 1)
        add_last(last, (0, 2, 4))
        finish(last - GROUP + 1, last)
        quantise(last, 0, PASSES // 2)
        multiply(last, 0, PASSES // 2)
        add_last(last, (6,))
        quantise(last, PASSES // 2)
        multiply(last, PASSES // 2)
        finish(last, UNITS)
